import numpy as np
import ml_dtypes


def mxq(x, axis, fmt="e4m3"):
    dtype, down = {"e4m3": (ml_dtypes.float8_e4m3fn, 7), "e5m2": (ml_dtypes.float8_e5m2, 14)}[fmt]
    v = np.moveaxis(np.asarray(x, np.float32).astype(ml_dtypes.bfloat16).astype(np.float64), axis, -1)
    blocks = v.reshape(v.shape[:-1] + (-1, 32))
    amax = np.abs(blocks).max(-1, keepdims=True)
    byte = np.maximum(np.where(amax > 0, np.frexp(amax)[1] - 1 + 127, 0) - down, 1)
    scale = np.exp2(byte - 127.0)
    codes = (blocks / scale).astype(np.float32).astype(dtype).astype(np.float64)
    return np.moveaxis((codes * scale).reshape(v.shape), -1, axis)


WIDE = False


def mx_kscale(k):
    if not WIDE:
        return np.ones(k)
    levels = np.array([10, -10, 5, -5, 0])
    if k % 512:
        return np.exp2(np.random.permutation(np.resize(levels, k // 32))).repeat(32)
    a = np.empty((k // 512, 16))
    for p in range(k // 512):
        a[p, :8] = np.random.permutation(np.resize(levels, 8))
        for g in range(8):
            far = levels[np.abs(levels - a[p, g]) >= 10]
            a[p, g + 8] = far[np.random.randint(len(far))]
    return np.exp2(a.ravel()).repeat(32)


BF16 = ml_dtypes.bfloat16


def bf(x):
    return np.asarray(x, np.float32).astype(BF16)


def f64(x):
    return np.asarray(x).astype(np.float64)


T, K, E, H, KVH, D = 512, 1024, 2048, 16, 4, 128
EPS = 1e-05


def rmsnorm(x, w):
    var = np.mean(np.square(x), axis=-1, keepdims=True)
    return x * (1.0 / np.sqrt(var + EPS)) * w


def setup_inputs():
    s = mx_kscale(E)
    return {"hidden_states": bf(np.random.standard_normal((T, E)) * s),
            "Wq": bf(np.random.standard_normal((H * D, E)) / np.sqrt(E) / s),
            "q_norm_w": bf(1.5 + 0.1 * np.random.standard_normal(D))}


def core(hidden_states, Wq, q_norm_w):
    q = mxq(f64(hidden_states), 1, "e4m3") @ mxq(f64(Wq), 1, "e4m3").T
    qh = rmsnorm(q.reshape(T, H, D), f64(q_norm_w))
    return qh.transpose(1, 0, 2)


def e4m3fn_bytes(y):
    return np.clip(np.asarray(y, np.float64), -448.0, 448.0).astype(np.float32).astype(ml_dtypes.float8_e4m3fn).view(np.uint8)


def reference(hidden_states, Wq, q_norm_w):
    out = core(hidden_states, Wq, q_norm_w)
    s = np.max(np.abs(out), axis=-1, keepdims=True) / 448.0
    return out, e4m3fn_bytes(out / s)

@@ -1,0 +1,336 @@
+from contextlib import ExitStack
+
+import concourse.mybir as mybir
+from concourse.masks import make_identity
+
+T, E, H, D = 512, 2048, 16, 128
+EPS = 1e-05
+FLOPS = 2 * T * E * H * D
+
+F32 = mybir.dt.float32
+BF16 = mybir.dt.bfloat16
+U32 = mybir.dt.uint32
+U8 = mybir.dt.uint8
+FP8X4 = mybir.dt.float8_e4m3fn_x4
+FP8 = mybir.dt.float8_e4m3fn
+ACT = mybir.ActivationFunctionType
+ALU = mybir.AluOpType
+AX = mybir.AxisListType
+
+P = 128
+PASSES = 4
+N_PAIRS = 10
+N_UNITS = 8
+LOAD_CHUNKS = (4, 2, 2, 2, 1, 1, 1, 1, 1, 1)
+HEAD_PAIRS = 4
+LOAD_ORDER = (0, 2, 1, 3, 4, 5, 6, 7, 8, 9)
+SCALAR_CASTS = 2
+BOTH = (0, 1)
+ALL = (0, 1, 2, 3)
+
+
+def tile_combcrossattention_pa_kernel(tc, hidden_states, Wq, q_norm_w, out_0, out_1):
+    nc = tc.nc
+    with ExitStack() as ctx:
+        const = ctx.enter_context(tc.tile_pool(name="const", bufs=1))
+        raw = ctx.enter_context(tc.tile_pool(name="raw", bufs=1))
+        stage = ctx.enter_context(tc.tile_pool(name="stage", bufs=8))
+        hcodes = ctx.enter_context(tc.tile_pool(name="hcodes", bufs=1))
+        wcodes = ctx.enter_context(tc.tile_pool(name="wcodes", bufs=3))
+        res = ctx.enter_context(tc.tile_pool(name="res", bufs=4))
+        small = ctx.enter_context(tc.tile_pool(name="small", bufs=5))
+        psum_t = ctx.enter_context(tc.psum_pool(name="psum_t", bufs=4))
+        psum_a = ctx.enter_context(tc.psum_pool(name="psum_a", bufs=4))
+
+        ident = const.tile([P, P], F32, name="ident")
+        make_identity(nc, ident[:])
+        one = const.tile([P, 1], F32, name="one")
+        nc.vector.memset(one[:], 1.0)
+        zero = const.tile([P, 1], F32, name="zero")
+        nc.vector.memset(zero[:], 0.0)
+        warm = const.tile([P, 1], F32, name="warm")
+        nc.scalar.activation(out=warm[:], in_=one[:], func=ACT.Abs_reciprocal_sqrt)
+
+        hv = hidden_states.rearrange("(m t) k -> m t k", t=4)
+        wv = Wq.rearrange("(i r) k -> r i k", r=P)
+        gain_row = const.tile([P, D], BF16, name="gain_row")
+        nc.vector.memset(gain_row[:], 0.0)
+        ones = const.tile([P, P], BF16, name="ones")
+        nc.vector.memset(ones[:], 1.0)
+        gain = const.tile([P, D], F32, name="gain")
+        chunks = {}
+        for pair in LOAD_ORDER:
+            if pair < 2:
+                src = hv[:, 2 * pair : 2 * pair + 2, :]
+            else:
+                src = wv[:, 2 * (pair - 2) : 2 * (pair - 2) + 2, :]
+            n_chunks = LOAD_CHUNKS[pair]
+            width = E // n_chunks
+            tiles = []
+            for c in range(n_chunks):
+                t = raw.tile([P, 2, width], BF16, name="raw%d_%d" % (pair, c))
+                nc.sync.dma_start(out=t[:], in_=src[:, :, width * c : width * (c + 1)])
+                tiles.append(t)
+            chunks[pair] = tiles
+            if pair == 0:
+                nc.sync.dma_start(out=gain_row[0:1, :], in_=q_norm_w.rearrange("(o d) -> o d", o=1))
+
+        banks = {}
+        staged = {}
+        codes = {}
+        scales = {}
+        accs = {}
+        stats = {}
+        outs = {}
+
+        def transposes(pair, passes):
+            per = PASSES // len(chunks[pair])
+            for g in passes:
+                xt = psum_t.tile([P, 2, 2, P], F32, name="xt", tag="xt")
+                chunk = chunks[pair][g // per]
+                base = 256 * (g % per)
+                for i in range(2):
+                    words = chunk[:, i, :].bitcast(F32)
+                    for u in range(2):
+                        nc.tensor.transpose(xt[:, i, u, :], words[:, base + u : base + 256 : 2], ident[:])
+                banks[(pair, g)] = xt
+
+        def copies(pair, passes):
+            for g in passes:
+                st = stage.tile([P, 1024], BF16, name="st", tag="st", align_bytes=64)
+                dst = st[:].bitcast(F32).rearrange("p (i r u) -> p i r u", i=2, u=2)
+                srcv = banks[(pair, g)][:].rearrange("p i u r -> p i r u")
+                if pair < HEAD_PAIRS and g == PASSES - 1:
+                    nc.vector.tensor_copy(out=dst, in_=srcv)
+                else:
+                    nc.scalar.copy(out=dst, in_=srcv)
+                staged[(pair, g)] = st
+
+        def quantize(pair, g):
+            if g == 0:
+                if pair < 2:
+                    codes[pair] = hcodes.tile([P, PASSES, 256], U32, name="hc%d" % pair, align_bytes=64)
+                    scales[pair] = hcodes.tile([P, PASSES, 256], U8, name="hs%d" % pair, align_bytes=64)
+                else:
+                    codes[pair] = wcodes.tile([P, PASSES, 256], U32, name="wc", tag="wc", align_bytes=64)
+                    scales[pair] = wcodes.tile([P, PASSES, 256], U8, name="ws", tag="ws", align_bytes=64)
+            nc.vector.quantize_mx(
+                out=codes[pair][:, g, :].bitcast(FP8X4), scales=scales[pair][:, g, :], in_=staged[(pair, g)][:]
+            )
+
+        def matmuls(n, which):
+            wc = codes[n + 2]
+            ws = scales[n + 2]
+            for b in which:
+                acc = psum_a.tile([P, 2, 256], F32, name="acc", tag="acc")
+                for tp in range(2):
+                    cols = slice(P * tp, P * (tp + 1))
+                    for g in range(PASSES):
+                        nc.tensor.matmul_mx(
+                            out=acc[:, tp, :],
+                            lhsT=codes[b][:, g, cols].bitcast(FP8X4),
+                            lhsT_scale=scales[b][:, g, cols],
+                            rhs=wc[:, g, :].bitcast(FP8X4),
+                            rhs_scale=ws[:, g, :],
+                            start=(g == 0),
+                            stop=(g == PASSES - 1),
+                        )
+                accs[(n, b)] = acc
+
+        def squares(n, b):
+            if b == 0:
+                ssq = small.tile([P, 8], F32, name="ssq", tag="ssq")
+                rstd = small.tile([P, 8], F32, name="rstd", tag="rstd")
+                amax = small.tile([P, 8], F32, name="amax", tag="amax")
+                rec = small.tile([P, 8], F32, name="rec", tag="rec")
+                fac = small.tile([P, 8], F32, name="fac", tag="fac")
+                stats[n] = (ssq, rstd, amax, rec, fac)
+            ssq, rstd = stats[n][0], stats[n][1]
+            acc = accs[(n, b)]
+            for tp in range(2):
+                for h in range(2):
+                    c = 4 * b + 2 * tp + h
+                    junk = small.tile([P, D], BF16, name="junk", tag="junk")
+                    nc.scalar.activation(
+                        out=junk[:], in_=acc[:, tp, D * h : D * (h + 1)], func=ACT.Square,
+                        accum_out=ssq[:, c : c + 1],
+                    )
+            nc.scalar.activation(
+                out=rstd[:, 4 * b : 4 * b + 4], in_=ssq[:, 4 * b : 4 * b + 4], func=ACT.Abs_reciprocal_sqrt,
+                scale=1.0 / D, bias=EPS,
+            )
+
+        def normalize(n, b):
+            if b == 0:
+                o0 = res.tile([P, 2, 4, D], F32, name="o0", tag="o0")
+                o1 = res.tile([P, 2, 4, D], FP8, name="o1", tag="o1")
+                outs[n] = (o0, o1)
+            o0 = outs[n][0]
+            rstd = stats[n][1]
+            acc = accs[(n, b)]
+            for tp in range(2):
+                for h in range(2):
+                    c = 4 * b + 2 * tp + h
+                    nc.vector.scalar_tensor_tensor(
+                        out=o0[:, h, 2 * b + tp, :], in0=acc[:, tp, D * h : D * (h + 1)],
+                        scalar=rstd[:, c : c + 1], in1=gain[:], op0=ALU.mult, op1=ALU.mult,
+                    )
+
+        def cols_of(tile8, which):
+            if len(which) == 2:
+                return tile8[:]
+            b = which[0]
+            return tile8[:].rearrange("p (h t) -> p h t", h=2)[:, :, 2 * b : 2 * b + 2]
+
+        def peak(n, which):
+            o0 = outs[n][0]
+            amax = stats[n][2]
+            if len(which) == 2:
+                nc.vector.tensor_reduce(
+                    out=amax[:], in_=o0[:].rearrange("p h t d -> p (h t) d"), axis=AX.X, op=ALU.max,
+                    apply_absolute_value=True,
+                )
+            else:
+                b = which[0]
+                for h in range(2):
+                    nc.vector.tensor_reduce(
+                        out=amax[:, 4 * h + 2 * b : 4 * h + 2 * b + 2], in_=o0[:, h, 2 * b : 2 * b + 2, :],
+                        axis=AX.X, op=ALU.max, apply_absolute_value=True,
+                    )
+
+        def inverse(n, which):
+            nc.vector.reciprocal(out=cols_of(stats[n][3], which), in_=cols_of(stats[n][2], which))
+
+        def factor(n, which):
+            nc.vector.tensor_scalar(
+                out=cols_of(stats[n][4], which), in0=cols_of(stats[n][3], which), scalar1=448.0, scalar2=None,
+                op0=ALU.mult,
+            )
+
+        def cast(n, h, t, on_vector):
+            o0, o1 = outs[n]
+            fac = stats[n][4]
+            c = 4 * h + t
+            if on_vector:
+                nc.vector.tensor_scalar(
+                    out=o1[:, h, t, :], in0=o0[:, h, t, :], scalar1=fac[:, c : c + 1], scalar2=None,
+                    op0=ALU.mult, saturate=False,
+                )
+            else:
+                nc.scalar.activation(
+                    out=o1[:, h, t, :], in_=o0[:, h, t, :], func=ACT.Identity,
+                    scale=fac[:, c : c + 1], bias=zero[:, 0:1], saturate=False,
+                )
+
+        def casts_vector(n):
+            for c in range(8 - SCALAR_CASTS):
+                cast(n, c // 4, c % 4, True)
+
+        def casts_scalar(n):
+            for c in range(8 - SCALAR_CASTS, 8):
+                cast(n, c // 4, c % 4, False)
+
+        def casts_bank(n, b, on_vector):
+            for h in range(2):
+                for tp in range(2):
+                    cast(n, h, 2 * b + tp, on_vector)
+
+        def store(n, which, dram, tile4):
+            lo, hi = 2 * which[0], 2 * which[-1] + 2
+            nc.sync.dma_start(
+                out=dram[2 * n : 2 * n + 2].rearrange("h (m t) d -> m h t d", t=4)[:, :, lo:hi, :].rearrange(
+                    "m h t d -> m h (t d)"
+                ),
+                in_=tile4[:, :, lo:hi, :].rearrange("p h t d -> p h (t d)"),
+            )
+
+        def store0(n, which):
+            store(n, which, out_0, outs[n][0])
+
+        def store1(n, which):
+            store(n, which, out_1, outs[n][1][:].bitcast(U8))
+
+        with tc.manual_schedule():
+            transposes(0, ALL)
+            copies(0, ALL)
+            transposes(2, ALL)
+            copies(2, ALL)
+            for g in ALL:
+                quantize(0, g)
+            transposes(1, ALL)
+            for g in ALL:
+                quantize(2, g)
+            copies(1, ALL)
+            spread = psum_a.tile([P, 2, 256], F32, name="acc", tag="acc")
+            nc.tensor.matmul(out=spread[:, 0, 0:D], lhsT=ones[:], rhs=gain_row[:], start=True, stop=True)
+            matmuls(0, (0,))
+            squares(0, 0)
+            for g in ALL:
+                quantize(1, g)
+            nc.vector.tensor_copy(out=gain[:], in_=spread[:, 0, 0:D])
+
+            for s in range(N_UNITS - 1):
+                nxt, u, v = s + 3, s - 1, s - 2
+                transposes(nxt, ALL)
+                if s == 0:
+                    matmuls(0, (1,))
+                else:
+                    matmuls(s, BOTH)
+                if u >= 0:
+                    squares(u, 1)
+                copies(nxt, ALL)
+                if v >= 0:
+                    casts_scalar(v)
+                if s > 0:
+                    squares(s, 0)
+                if u >= 0:
+                    normalize(u, 0)
+                if v >= 0:
+                    casts_vector(v)
+                    store1(v, BOTH)
+                if u >= 0:
+                    normalize(u, 1)
+                    store0(u, BOTH)
+                quantize(nxt, 0)
+                if u >= 0:
+                    peak(u, BOTH)
+                quantize(nxt, 1)
+                if u >= 0:
+                    inverse(u, BOTH)
+                quantize(nxt, 2)
+                if u >= 0:
+                    factor(u, BOTH)
+                quantize(nxt, 3)
+
+            matmuls(7, BOTH)
+            squares(6, 1)
+            squares(7, 0)
+            casts_scalar(5)
+            squares(7, 1)
+            normalize(6, 0)
+            casts_vector(5)
+            store1(5, BOTH)
+            peak(6, (0,))
+            normalize(6, 1)
+            store0(6, BOTH)
+            inverse(6, (0,))
+            normalize(7, 0)
+            store0(7, (0,))
+            factor(6, (0,))
+            peak(6, (1,))
+            casts_bank(6, 0, False)
+            normalize(7, 1)
+            store0(7, (1,))
+            inverse(6, (1,))
+            peak(7, (0,))
+            factor(6, (1,))
+            peak(7, (1,))
+            casts_bank(6, 1, False)
+            store1(6, BOTH)
+            inverse(7, (0,))
+            inverse(7, (1,))
+            factor(7, (0,))
+            factor(7, (1,))
+            casts_bank(7, 0, False)
+            casts_bank(7, 1, True)
+            store1(7, BOTH)

@@ -155,6 +155,9 @@ def tile_combcrossattention_pa_kernel(tc, hidden_states, Wq, q_norm_w, out_0, ou
                         out=junk[:], in_=acc[:, tp, D * h : D * (h + 1)], func=ACT.Square,
                         accum_out=ssq[:, c : c + 1],
                     )
+
+        def rsqrt(n, b):
+            ssq, rstd = stats[n][0], stats[n][1]
             nc.scalar.activation(
                 out=rstd[:, 4 * b : 4 * b + 4], in_=ssq[:, 4 * b : 4 * b + 4], func=ACT.Abs_reciprocal_sqrt,
                 scale=1.0 / D, bias=EPS,
@@ -226,8 +229,8 @@ def tile_combcrossattention_pa_kernel(tc, hidden_states, Wq, q_norm_w, out_0, ou
             for c in range(8 - SCALAR_CASTS):
                 cast(n, c // 4, c % 4, True)
 
-        def casts_scalar(n):
-            for c in range(8 - SCALAR_CASTS, 8):
+        def casts_scalar(n, which):
+            for c in which:
                 cast(n, c // 4, c % 4, False)
 
         def casts_bank(n, b, on_vector):
@@ -278,11 +281,20 @@ def tile_combcrossattention_pa_kernel(tc, hidden_states, Wq, q_norm_w, out_0, ou
                     matmuls(s, BOTH)
                 if u >= 0:
                     squares(u, 1)
-                copies(nxt, ALL)
+                copies(nxt, (0,))
+                if u >= 0:
+                    rsqrt(u, 1)
+                else:
+                    rsqrt(0, 0)
+                copies(nxt, (1, 2, 3))
                 if v >= 0:
-                    casts_scalar(v)
+                    casts_scalar(v, (6,))
                 if s > 0:
                     squares(s, 0)
+                if v >= 0:
+                    casts_scalar(v, (7,))
+                if s > 0:
+                    rsqrt(s, 0)
                 if u >= 0:
                     normalize(u, 0)
                 if v >= 0:
@@ -304,9 +316,13 @@ def tile_combcrossattention_pa_kernel(tc, hidden_states, Wq, q_norm_w, out_0, ou
 
             matmuls(7, BOTH)
             squares(6, 1)
+            casts_scalar(5, (6,))
+            rsqrt(6, 1)
             squares(7, 0)
-            casts_scalar(5)
+            casts_scalar(5, (7,))
+            rsqrt(7, 0)
             squares(7, 1)
+            rsqrt(7, 1)
             normalize(6, 0)
             casts_vector(5)
             store1(5, BOTH)

@@ -24,7 +24,7 @@ N_UNITS = 8
 LOAD_CHUNKS = (4, 2, 2, 2, 1, 1, 1, 1, 1, 1)
 HEAD_PAIRS = 4
 LOAD_ORDER = (0, 2, 1, 3, 4, 5, 6, 7, 8, 9)
-SCALAR_CASTS = 2
+SCALAR_CASTS = 0
 BOTH = (0, 1)
 ALL = (0, 1, 2, 3)
 
@@ -229,10 +229,6 @@ def tile_combcrossattention_pa_kernel(tc, hidden_states, Wq, q_norm_w, out_0, ou
             for c in range(8 - SCALAR_CASTS):
                 cast(n, c // 4, c % 4, True)
 
-        def casts_scalar(n, which):
-            for c in which:
-                cast(n, c // 4, c % 4, False)
-
         def casts_bank(n, b, on_vector):
             for h in range(2):
                 for tp in range(2):
@@ -287,13 +283,8 @@ def tile_combcrossattention_pa_kernel(tc, hidden_states, Wq, q_norm_w, out_0, ou
                 else:
                     rsqrt(0, 0)
                 copies(nxt, (1, 2, 3))
-                if v >= 0:
-                    casts_scalar(v, (6,))
                 if s > 0:
                     squares(s, 0)
-                if v >= 0:
-                    casts_scalar(v, (7,))
-                if s > 0:
                     rsqrt(s, 0)
                 if u >= 0:
                     normalize(u, 0)
@@ -316,10 +307,8 @@ def tile_combcrossattention_pa_kernel(tc, hidden_states, Wq, q_norm_w, out_0, ou
 
             matmuls(7, BOTH)
             squares(6, 1)
-            casts_scalar(5, (6,))
             rsqrt(6, 1)
             squares(7, 0)
-            casts_scalar(5, (7,))
             rsqrt(7, 0)
             squares(7, 1)
             rsqrt(7, 1)

@@ -21,7 +21,7 @@ P = 128
 PASSES = 4
 N_PAIRS = 10
 N_UNITS = 8
-LOAD_CHUNKS = (4, 2, 2, 2, 1, 1, 1, 1, 1, 1)
+TILE_CHUNKS = {(0, 0): 2, (1, 1): 2}
 HEAD_PAIRS = 4
 LOAD_ORDER = (0, 2, 1, 3, 4, 5, 6, 7, 8, 9)
 SCALAR_CASTS = 0
@@ -34,7 +34,7 @@ def tile_combcrossattention_pa_kernel(tc, hidden_states, Wq, q_norm_w, out_0, ou
     with ExitStack() as ctx:
         const = ctx.enter_context(tc.tile_pool(name="const", bufs=1))
         raw = ctx.enter_context(tc.tile_pool(name="raw", bufs=1))
-        stage = ctx.enter_context(tc.tile_pool(name="stage", bufs=8))
+        stage = ctx.enter_context(tc.tile_pool(name="stage", bufs=3))
         hcodes = ctx.enter_context(tc.tile_pool(name="hcodes", bufs=1))
         wcodes = ctx.enter_context(tc.tile_pool(name="wcodes", bufs=3))
         res = ctx.enter_context(tc.tile_pool(name="res", bufs=4))
@@ -58,20 +58,30 @@ def tile_combcrossattention_pa_kernel(tc, hidden_states, Wq, q_norm_w, out_0, ou
         ones = const.tile([P, P], BF16, name="ones")
         nc.vector.memset(ones[:], 1.0)
         gain = const.tile([P, D], F32, name="gain")
-        chunks = {}
+        raw_words = {}
         for pair in LOAD_ORDER:
-            if pair < 2:
-                src = hv[:, 2 * pair : 2 * pair + 2, :]
+            if pair < HEAD_PAIRS:
+                for i in range(2):
+                    if pair < 2:
+                        src = hv[:, 2 * pair + i, :]
+                    else:
+                        src = wv[:, 2 * (pair - 2) + i, :]
+                    n_chunks = TILE_CHUNKS.get((pair, i), 1)
+                    width = E // n_chunks
+                    per = PASSES // n_chunks
+                    for c in range(n_chunks):
+                        t = raw.tile([P, width], BF16, name="raw%d_%d_%d" % (pair, i, c))
+                        nc.sync.dma_start(out=t[:], in_=src[:, width * c : width * (c + 1)])
+                        words = t[:].bitcast(F32)
+                        for k in range(per):
+                            raw_words[(pair, i, per * c + k)] = words[:, 256 * k : 256 * (k + 1)]
             else:
-                src = wv[:, 2 * (pair - 2) : 2 * (pair - 2) + 2, :]
-            n_chunks = LOAD_CHUNKS[pair]
-            width = E // n_chunks
-            tiles = []
-            for c in range(n_chunks):
-                t = raw.tile([P, 2, width], BF16, name="raw%d_%d" % (pair, c))
-                nc.sync.dma_start(out=t[:], in_=src[:, :, width * c : width * (c + 1)])
-                tiles.append(t)
-            chunks[pair] = tiles
+                t = raw.tile([P, 2, E], BF16, name="raw%d" % pair)
+                nc.sync.dma_start(out=t[:], in_=wv[:, 2 * (pair - 2) : 2 * (pair - 2) + 2, :])
+                for i in range(2):
+                    words = t[:, i, :].bitcast(F32)
+                    for g in range(PASSES):
+                        raw_words[(pair, i, g)] = words[:, 256 * g : 256 * (g + 1)]
             if pair == 0:
                 nc.sync.dma_start(out=gain_row[0:1, :], in_=q_norm_w.rearrange("(o d) -> o d", o=1))
 
@@ -83,28 +93,33 @@ def tile_combcrossattention_pa_kernel(tc, hidden_states, Wq, q_norm_w, out_0, ou
         stats = {}
         outs = {}
 
-        def transposes(pair, passes):
-            per = PASSES // len(chunks[pair])
-            for g in passes:
-                xt = psum_t.tile([P, 2, 2, P], F32, name="xt", tag="xt")
-                chunk = chunks[pair][g // per]
-                base = 256 * (g % per)
-                for i in range(2):
-                    words = chunk[:, i, :].bitcast(F32)
-                    for u in range(2):
-                        nc.tensor.transpose(xt[:, i, u, :], words[:, base + u : base + 256 : 2], ident[:])
-                banks[(pair, g)] = xt
+        def bank_of(pair, b4):
+            if pair < HEAD_PAIRS:
+                return b4 // 2, b4 % 2
+            return b4 % 2, b4 // 2
 
-        def copies(pair, passes):
-            for g in passes:
-                st = stage.tile([P, 1024], BF16, name="st", tag="st", align_bytes=64)
-                dst = st[:].bitcast(F32).rearrange("p (i r u) -> p i r u", i=2, u=2)
-                srcv = banks[(pair, g)][:].rearrange("p i u r -> p i r u")
-                if pair < HEAD_PAIRS and g == PASSES - 1:
+        def transposes(pair, which):
+            for b4 in which:
+                i, j = bank_of(pair, b4)
+                xt = psum_t.tile([P, 2, 2, P], F32, name="xt", tag="xt")
+                for gp in range(2):
+                    words = raw_words[(pair, i, 2 * j + gp)]
+                    for u in range(2):
+                        nc.tensor.transpose(xt[:, gp, u, :], words[:, u:256:2], ident[:])
+                banks[(pair, b4)] = xt
+
+        def copies(pair, which):
+            for b4 in which:
+                i, j = bank_of(pair, b4)
+                if b4 == 0:
+                    staged[pair] = stage.tile([P, PASSES * 1024], BF16, name="st", tag="st", align_bytes=64)
+                view = staged[pair][:].bitcast(F32).rearrange("p (g i r u) -> p g i r u", g=PASSES, i=2, u=2)
+                dst = view[:, 2 * j : 2 * j + 2, i, :, :]
+                srcv = banks[(pair, b4)][:].rearrange("p g u r -> p g r u")
+                if pair < HEAD_PAIRS and b4 == PASSES - 1:
                     nc.vector.tensor_copy(out=dst, in_=srcv)
                 else:
                     nc.scalar.copy(out=dst, in_=srcv)
-                staged[(pair, g)] = st
 
         def quantize(pair, g):
             if g == 0:
@@ -115,7 +130,7 @@ def tile_combcrossattention_pa_kernel(tc, hidden_states, Wq, q_norm_w, out_0, ou
                     codes[pair] = wcodes.tile([P, PASSES, 256], U32, name="wc", tag="wc", align_bytes=64)
                     scales[pair] = wcodes.tile([P, PASSES, 256], U8, name="ws", tag="ws", align_bytes=64)
             nc.vector.quantize_mx(
-                out=codes[pair][:, g, :].bitcast(FP8X4), scales=scales[pair][:, g, :], in_=staged[(pair, g)][:]
+                out=codes[pair][:, g, :].bitcast(FP8X4), scales=scales[pair][:, g, :], in_=staged[pair][:, 1024 * g : 1024 * (g + 1)]
             )
 
         def matmuls(n, which):

@@ -268,9 +268,9 @@ def tile_combcrossattention_pa_kernel(tc, hidden_states, Wq, q_norm_w, out_0, ou
             transposes(0, ALL)
             copies(0, ALL)
             transposes(2, ALL)
-            copies(2, ALL)
             for g in ALL:
                 quantize(0, g)
+            copies(2, ALL)
             transposes(1, ALL)
             for g in ALL:
                 quantize(2, g)

@@ -21,7 +21,6 @@ P = 128
 PASSES = 4
 N_PAIRS = 10
 N_UNITS = 8
-TILE_CHUNKS = {(0, 0): 2, (1, 1): 2}
 HEAD_PAIRS = 4
 LOAD_ORDER = (0, 2, 1, 3, 4, 5, 6, 7, 8, 9)
 SCALAR_CASTS = 0
@@ -66,15 +65,11 @@ def tile_combcrossattention_pa_kernel(tc, hidden_states, Wq, q_norm_w, out_0, ou
                         src = hv[:, 2 * pair + i, :]
                     else:
                         src = wv[:, 2 * (pair - 2) + i, :]
-                    n_chunks = TILE_CHUNKS.get((pair, i), 1)
-                    width = E // n_chunks
-                    per = PASSES // n_chunks
-                    for c in range(n_chunks):
-                        t = raw.tile([P, width], BF16, name="raw%d_%d_%d" % (pair, i, c))
-                        nc.sync.dma_start(out=t[:], in_=src[:, width * c : width * (c + 1)])
-                        words = t[:].bitcast(F32)
-                        for k in range(per):
-                            raw_words[(pair, i, per * c + k)] = words[:, 256 * k : 256 * (k + 1)]
+                    t = raw.tile([P, E], BF16, name="raw%d_%d" % (pair, i))
+                    nc.sync.dma_start(out=t[:], in_=src)
+                    words = t[:].bitcast(F32)
+                    for g in range(PASSES):
+                        raw_words[(pair, i, g)] = words[:, 256 * g : 256 * (g + 1)]
             else:
                 t = raw.tile([P, 2, E], BF16, name="raw%d" % pair)
                 nc.sync.dma_start(out=t[:], in_=wv[:, 2 * (pair - 2) : 2 * (pair - 2) + 2, :])

@@ -23,7 +23,6 @@ N_PAIRS = 10
 N_UNITS = 8
 HEAD_PAIRS = 4
 LOAD_ORDER = (0, 2, 1, 3, 4, 5, 6, 7, 8, 9)
-SCALAR_CASTS = 0
 BOTH = (0, 1)
 ALL = (0, 1, 2, 3)
 
@@ -214,6 +213,9 @@ def tile_combcrossattention_pa_kernel(tc, hidden_states, Wq, q_norm_w, out_0, ou
         def inverse(n, which):
             nc.vector.reciprocal(out=cols_of(stats[n][3], which), in_=cols_of(stats[n][2], which))
 
+        def factor_scalar(n, which):
+            nc.scalar.mul(out=cols_of(stats[n][4], which), in_=cols_of(stats[n][3], which), mul=448.0)
+
         def factor(n, which):
             nc.vector.tensor_scalar(
                 out=cols_of(stats[n][4], which), in0=cols_of(stats[n][3], which), scalar1=448.0, scalar2=None,
@@ -235,9 +237,9 @@ def tile_combcrossattention_pa_kernel(tc, hidden_states, Wq, q_norm_w, out_0, ou
                     scale=fac[:, c : c + 1], bias=zero[:, 0:1], saturate=False,
                 )
 
-        def casts_vector(n):
-            for c in range(8 - SCALAR_CASTS):
-                cast(n, c // 4, c % 4, True)
+        def casts(n, which, on_vector):
+            for c in which:
+                cast(n, c // 4, c % 4, on_vector)
 
         def casts_bank(n, b, on_vector):
             for h in range(2):
@@ -285,27 +287,35 @@ def tile_combcrossattention_pa_kernel(tc, hidden_states, Wq, q_norm_w, out_0, ou
                     matmuls(0, (1,))
                 else:
                     matmuls(s, BOTH)
+                last = s == N_UNITS - 2
                 if u >= 0:
                     squares(u, 1)
-                copies(nxt, (0,))
+                if last:
+                    casts(v, (7,), False)
+                else:
+                    copies(nxt, (0,))
                 if u >= 0:
                     rsqrt(u, 1)
                 else:
                     rsqrt(0, 0)
-                copies(nxt, (1, 2, 3))
+                copies(nxt, ALL if last else (1, 2, 3))
                 if s > 0:
                     squares(s, 0)
                     rsqrt(s, 0)
                 if u >= 0:
                     normalize(u, 0)
                 if v >= 0:
-                    casts_vector(v)
+                    casts(v, (0, 1, 2, 3, 4, 5, 6) if last else (0, 1, 2, 3, 4, 5, 6, 7), True)
                     store1(v, BOTH)
                 if u >= 0:
                     normalize(u, 1)
                     store0(u, BOTH)
+                if last:
+                    peak(u, (0,))
                 quantize(nxt, 0)
-                if u >= 0:
+                if last:
+                    peak(u, (1,))
+                elif u >= 0:
                     peak(u, BOTH)
                 quantize(nxt, 1)
                 if u >= 0:
@@ -317,35 +327,41 @@ def tile_combcrossattention_pa_kernel(tc, hidden_states, Wq, q_norm_w, out_0, ou
 
             matmuls(7, BOTH)
             squares(6, 1)
+            casts(5, (4,), False)
             rsqrt(6, 1)
+            casts(5, (5, 6), False)
             squares(7, 0)
             rsqrt(7, 0)
             squares(7, 1)
+            casts(5, (7,), False)
             rsqrt(7, 1)
+            casts(5, (0, 1), True)
             normalize(6, 0)
-            casts_vector(5)
-            store1(5, BOTH)
+            casts(5, (2, 3), True)
             peak(6, (0,))
             normalize(6, 1)
             store0(6, BOTH)
+            store1(5, BOTH)
             inverse(6, (0,))
+            peak(6, (1,))
+            factor(6, (0,))
             normalize(7, 0)
             store0(7, (0,))
-            factor(6, (0,))
-            peak(6, (1,))
             casts_bank(6, 0, False)
+            inverse(6, (1,))
             normalize(7, 1)
             store0(7, (1,))
-            inverse(6, (1,))
-            peak(7, (0,))
             factor(6, (1,))
+            peak(7, (0,))
             peak(7, (1,))
-            casts_bank(6, 1, False)
-            store1(6, BOTH)
+            casts(6, (2, 3), False)
             inverse(7, (0,))
+            factor_scalar(7, (0,))
+            casts(6, (6,), False)
             inverse(7, (1,))
-            factor(7, (0,))
-            factor(7, (1,))
-            casts_bank(7, 0, False)
+            factor_scalar(7, (1,))
+            casts(6, (7,), False)
+            store1(6, BOTH)
+            casts_bank(7, 0, True)
             casts_bank(7, 1, True)
             store1(7, BOTH)

@@ -261,8 +261,44 @@ def tile_combcrossattention_pa_kernel(tc, hidden_states, Wq, q_norm_w, out_0, ou
         def store1(n, which):
             store(n, which, out_1, outs[n][1][:].bitcast(U8))
 
+        y_last = const.tile([P, 4, D], F32, name="y_last")
+        last_stats = const.tile([P, 3, 4], F32, name="last_stats")
+
+        def gain_last():
+            nc.vector.tensor_tensor(
+                out=y_last[:], in0=accs[(7, 1)][:].rearrange("p t (h d) -> p (t h) d", h=2),
+                in1=gain[:].unsqueeze(1).broadcast_to([P, 4, D]), op=ALU.mult,
+            )
+
+        def scale_last():
+            for c in range(4):
+                nc.scalar.activation(
+                    out=outs[7][0][:, c % 2, 2 + c // 2, :], in_=y_last[:, c, :], func=ACT.Copy,
+                    scale=stats[7][1][:, 4 + c : 5 + c],
+                )
+
+        def peak_last():
+            nc.vector.tensor_reduce(
+                out=last_stats[:, 0, :], in_=y_last[:], axis=AX.X, op=ALU.max, apply_absolute_value=True,
+            )
+
+        def inverse_last():
+            nc.vector.reciprocal(out=last_stats[:, 1, :], in_=last_stats[:, 0, :])
+
+        def factor_last():
+            nc.scalar.mul(out=last_stats[:, 2, :], in_=last_stats[:, 1, :], mul=448.0)
+
+        def casts_last():
+            for c in range(4):
+                nc.vector.tensor_scalar(
+                    out=outs[7][1][:, c % 2, 2 + c // 2, :], in0=y_last[:, c, :], scalar1=last_stats[:, 2, c : c + 1],
+                    scalar2=None, op0=ALU.mult, saturate=False,
+                )
+
         with tc.manual_schedule():
             transposes(0, ALL)
+            spread = psum_a.tile([P, 2, 256], F32, name="acc", tag="acc")
+            nc.tensor.matmul(out=spread[:, 0, 0:D], lhsT=ones[:], rhs=gain_row[:], start=True, stop=True)
             copies(0, ALL)
             transposes(2, ALL)
             for g in ALL:
@@ -272,8 +308,6 @@ def tile_combcrossattention_pa_kernel(tc, hidden_states, Wq, q_norm_w, out_0, ou
             for g in ALL:
                 quantize(2, g)
             copies(1, ALL)
-            spread = psum_a.tile([P, 2, 256], F32, name="acc", tag="acc")
-            nc.tensor.matmul(out=spread[:, 0, 0:D], lhsT=ones[:], rhs=gain_row[:], start=True, stop=True)
             matmuls(0, (0,))
             squares(0, 0)
             for g in ALL:
@@ -347,21 +381,23 @@ def tile_combcrossattention_pa_kernel(tc, hidden_states, Wq, q_norm_w, out_0, ou
             factor(6, (0,))
             normalize(7, 0)
             store0(7, (0,))
-            casts_bank(6, 0, False)
+            casts(6, (0,), False)
             inverse(6, (1,))
-            normalize(7, 1)
+            gain_last()
+            scale_last()
             store0(7, (1,))
+            casts(6, (1, 4), False)
             factor(6, (1,))
             peak(7, (0,))
-            peak(7, (1,))
-            casts(6, (2, 3), False)
+            peak_last()
             inverse(7, (0,))
             factor_scalar(7, (0,))
-            casts(6, (6,), False)
-            inverse(7, (1,))
-            factor_scalar(7, (1,))
-            casts(6, (7,), False)
+            casts(6, (5,), False)
+            casts(6, (6, 7), True)
+            inverse_last()
+            factor_last()
+            casts(6, (2, 3), False)
             store1(6, BOTH)
             casts_bank(7, 0, True)
-            casts_bank(7, 1, True)
+            casts_last()
             store1(7, BOTH)

@@ -297,8 +297,6 @@ def tile_combcrossattention_pa_kernel(tc, hidden_states, Wq, q_norm_w, out_0, ou
 
         with tc.manual_schedule():
             transposes(0, ALL)
-            spread = psum_a.tile([P, 2, 256], F32, name="acc", tag="acc")
-            nc.tensor.matmul(out=spread[:, 0, 0:D], lhsT=ones[:], rhs=gain_row[:], start=True, stop=True)
             copies(0, ALL)
             transposes(2, ALL)
             for g in ALL:
@@ -308,6 +306,8 @@ def tile_combcrossattention_pa_kernel(tc, hidden_states, Wq, q_norm_w, out_0, ou
             for g in ALL:
                 quantize(2, g)
             copies(1, ALL)
+            spread = psum_a.tile([P, 2, 256], F32, name="acc", tag="acc")
+            nc.tensor.matmul(out=spread[:, 0, 0:D], lhsT=ones[:], rhs=gain_row[:], start=True, stop=True)
             matmuls(0, (0,))
             squares(0, 0)
             for g in ALL:

from contextlib import ExitStack

import concourse.mybir as mybir
from concourse.masks import make_identity

T, E, H, D = 512, 2048, 16, 128
EPS = 1e-05
FLOPS = 2 * T * E * H * D

F32 = mybir.dt.float32
BF16 = mybir.dt.bfloat16
U32 = mybir.dt.uint32
U8 = mybir.dt.uint8
FP8X4 = mybir.dt.float8_e4m3fn_x4
FP8 = mybir.dt.float8_e4m3fn
ACT = mybir.ActivationFunctionType
ALU = mybir.AluOpType
AX = mybir.AxisListType

P = 128
PASSES = 4
N_PAIRS = 10
N_UNITS = 8
HEAD_PAIRS = 4
LOAD_ORDER = (0, 2, 1, 3, 4, 5, 6, 7, 8, 9)
BOTH = (0, 1)
ALL = (0, 1, 2, 3)


def tile_combcrossattention_pa_kernel(tc, hidden_states, Wq, q_norm_w, out_0, out_1):
    nc = tc.nc
    with ExitStack() as ctx:
        const = ctx.enter_context(tc.tile_pool(name="const", bufs=1))
        raw = ctx.enter_context(tc.tile_pool(name="raw", bufs=1))
        stage = ctx.enter_context(tc.tile_pool(name="stage", bufs=3))
        hcodes = ctx.enter_context(tc.tile_pool(name="hcodes", bufs=1))
        wcodes = ctx.enter_context(tc.tile_pool(name="wcodes", bufs=3))
        res = ctx.enter_context(tc.tile_pool(name="res", bufs=4))
        small = ctx.enter_context(tc.tile_pool(name="small", bufs=5))
        psum_t = ctx.enter_context(tc.psum_pool(name="psum_t", bufs=4))
        psum_a = ctx.enter_context(tc.psum_pool(name="psum_a", bufs=4))

        ident = const.tile([P, P], F32, name="ident")
        make_identity(nc, ident[:])
        one = const.tile([P, 1], F32, name="one")
        nc.vector.memset(one[:], 1.0)
        zero = const.tile([P, 1], F32, name="zero")
        nc.vector.memset(zero[:], 0.0)
        warm = const.tile([P, 1], F32, name="warm")
        nc.scalar.activation(out=warm[:], in_=one[:], func=ACT.Abs_reciprocal_sqrt)

        hv = hidden_states.rearrange("(m t) k -> m t k", t=4)
        wv = Wq.rearrange("(i r) k -> r i k", r=P)
        gain_row = const.tile([P, D], BF16, name="gain_row")
        nc.vector.memset(gain_row[:], 0.0)
        ones = const.tile([P, P], BF16, name="ones")
        nc.vector.memset(ones[:], 1.0)
        gain = const.tile([P, D], F32, name="gain")
        raw_words = {}
        for pair in LOAD_ORDER:
            if pair < HEAD_PAIRS:
                for i in range(2):
                    if pair < 2:
                        src = hv[:, 2 * pair + i, :]
                    else:
                        src = wv[:, 2 * (pair - 2) + i, :]
                    t = raw.tile([P, E], BF16, name="raw%d_%d" % (pair, i))
                    nc.sync.dma_start(out=t[:], in_=src)
                    words = t[:].bitcast(F32)
                    for g in range(PASSES):
                        raw_words[(pair, i, g)] = words[:, 256 * g : 256 * (g + 1)]
            else:
                t = raw.tile([P, 2, E], BF16, name="raw%d" % pair)
                nc.sync.dma_start(out=t[:], in_=wv[:, 2 * (pair - 2) : 2 * (pair - 2) + 2, :])
                for i in range(2):
                    words = t[:, i, :].bitcast(F32)
                    for g in range(PASSES):
                        raw_words[(pair, i, g)] = words[:, 256 * g : 256 * (g + 1)]
            if pair == 0:
                nc.sync.dma_start(out=gain_row[0:1, :], in_=q_norm_w.rearrange("(o d) -> o d", o=1))

        banks = {}
        staged = {}
        codes = {}
        scales = {}
        accs = {}
        stats = {}
        outs = {}

        def bank_of(pair, b4):
            if pair < HEAD_PAIRS:
                return b4 // 2, b4 % 2
            return b4 % 2, b4 // 2

        def transposes(pair, which):
            for b4 in which:
                i, j = bank_of(pair, b4)
                xt = psum_t.tile([P, 2, 2, P], F32, name="xt", tag="xt")
                for gp in range(2):
                    words = raw_words[(pair, i, 2 * j + gp)]
                    for u in range(2):
                        nc.tensor.transpose(xt[:, gp, u, :], words[:, u:256:2], ident[:])
                banks[(pair, b4)] = xt

        def copies(pair, which):
            for b4 in which:
                i, j = bank_of(pair, b4)
                if b4 == 0:
                    staged[pair] = stage.tile([P, PASSES * 1024], BF16, name="st", tag="st", align_bytes=64)
                view = staged[pair][:].bitcast(F32).rearrange("p (g i r u) -> p g i r u", g=PASSES, i=2, u=2)
                dst = view[:, 2 * j : 2 * j + 2, i, :, :]
                srcv = banks[(pair, b4)][:].rearrange("p g u r -> p g r u")
                if pair < HEAD_PAIRS and b4 == PASSES - 1:
                    nc.vector.tensor_copy(out=dst, in_=srcv)
                else:
                    nc.scalar.copy(out=dst, in_=srcv)

        def quantize(pair, g):
            if g == 0:
                if pair < 2:
                    codes[pair] = hcodes.tile([P, PASSES, 256], U32, name="hc%d" % pair, align_bytes=64)
                    scales[pair] = hcodes.tile([P, PASSES, 256], U8, name="hs%d" % pair, align_bytes=64)
                else:
                    codes[pair] = wcodes.tile([P, PASSES, 256], U32, name="wc", tag="wc", align_bytes=64)
                    scales[pair] = wcodes.tile([P, PASSES, 256], U8, name="ws", tag="ws", align_bytes=64)
            nc.vector.quantize_mx(
                out=codes[pair][:, g, :].bitcast(FP8X4), scales=scales[pair][:, g, :], in_=staged[pair][:, 1024 * g : 1024 * (g + 1)]
            )

        def matmuls(n, which):
            wc = codes[n + 2]
            ws = scales[n + 2]
            for b in which:
                acc = psum_a.tile([P, 2, 256], F32, name="acc", tag="acc")
                for tp in range(2):
                    cols = slice(P * tp, P * (tp + 1))
                    for g in range(PASSES):
                        nc.tensor.matmul_mx(
                            out=acc[:, tp, :],
                            lhsT=codes[b][:, g, cols].bitcast(FP8X4),
                            lhsT_scale=scales[b][:, g, cols],
                            rhs=wc[:, g, :].bitcast(FP8X4),
                            rhs_scale=ws[:, g, :],
                            start=(g == 0),
                            stop=(g == PASSES - 1),
                        )
                accs[(n, b)] = acc

        def squares(n, b):
            if b == 0:
                ssq = small.tile([P, 8], F32, name="ssq", tag="ssq")
                rstd = small.tile([P, 8], F32, name="rstd", tag="rstd")
                amax = small.tile([P, 8], F32, name="amax", tag="amax")
                rec = small.tile([P, 8], F32, name="rec", tag="rec")
                fac = small.tile([P, 8], F32, name="fac", tag="fac")
                stats[n] = (ssq, rstd, amax, rec, fac)
            ssq, rstd = stats[n][0], stats[n][1]
            acc = accs[(n, b)]
            for tp in range(2):
                for h in range(2):
                    c = 4 * b + 2 * tp + h
                    junk = small.tile([P, D], BF16, name="junk", tag="junk")
                    nc.scalar.activation(
                        out=junk[:], in_=acc[:, tp, D * h : D * (h + 1)], func=ACT.Square,
                        accum_out=ssq[:, c : c + 1],
                    )

        def rsqrt(n, b):
            ssq, rstd = stats[n][0], stats[n][1]
            nc.scalar.activation(
                out=rstd[:, 4 * b : 4 * b + 4], in_=ssq[:, 4 * b : 4 * b + 4], func=ACT.Abs_reciprocal_sqrt,
                scale=1.0 / D, bias=EPS,
            )

        def normalize(n, b):
            if b == 0:
                o0 = res.tile([P, 2, 4, D], F32, name="o0", tag="o0")
                o1 = res.tile([P, 2, 4, D], FP8, name="o1", tag="o1")
                outs[n] = (o0, o1)
            o0 = outs[n][0]
            rstd = stats[n][1]
            acc = accs[(n, b)]
            for tp in range(2):
                for h in range(2):
                    c = 4 * b + 2 * tp + h
                    nc.vector.scalar_tensor_tensor(
                        out=o0[:, h, 2 * b + tp, :], in0=acc[:, tp, D * h : D * (h + 1)],
                        scalar=rstd[:, c : c + 1], in1=gain[:], op0=ALU.mult, op1=ALU.mult,
                    )

        def cols_of(tile8, which):
            if len(which) == 2:
                return tile8[:]
            b = which[0]
            return tile8[:].rearrange("p (h t) -> p h t", h=2)[:, :, 2 * b : 2 * b + 2]

        def peak(n, which):
            o0 = outs[n][0]
            amax = stats[n][2]
            if len(which) == 2:
                nc.vector.tensor_reduce(
                    out=amax[:], in_=o0[:].rearrange("p h t d -> p (h t) d"), axis=AX.X, op=ALU.max,
                    apply_absolute_value=True,
                )
            else:
                b = which[0]
                for h in range(2):
                    nc.vector.tensor_reduce(
                        out=amax[:, 4 * h + 2 * b : 4 * h + 2 * b + 2], in_=o0[:, h, 2 * b : 2 * b + 2, :],
                        axis=AX.X, op=ALU.max, apply_absolute_value=True,
                    )

        def inverse(n, which):
            nc.vector.reciprocal(out=cols_of(stats[n][3], which), in_=cols_of(stats[n][2], which))

        def factor_scalar(n, which):
            nc.scalar.mul(out=cols_of(stats[n][4], which), in_=cols_of(stats[n][3], which), mul=448.0)

        def factor(n, which):
            nc.vector.tensor_scalar(
                out=cols_of(stats[n][4], which), in0=cols_of(stats[n][3], which), scalar1=448.0, scalar2=None,
                op0=ALU.mult,
            )

        def cast(n, h, t, on_vector):
            o0, o1 = outs[n]
            fac = stats[n][4]
            c = 4 * h + t
            if on_vector:
                nc.vector.tensor_scalar(
                    out=o1[:, h, t, :], in0=o0[:, h, t, :], scalar1=fac[:, c : c + 1], scalar2=None,
                    op0=ALU.mult, saturate=False,
                )
            else:
                nc.scalar.activation(
                    out=o1[:, h, t, :], in_=o0[:, h, t, :], func=ACT.Identity,
                    scale=fac[:, c : c + 1], bias=zero[:, 0:1], saturate=False,
                )

        def casts(n, which, on_vector):
            for c in which:
                cast(n, c // 4, c % 4, on_vector)

        def casts_bank(n, b, on_vector):
            for h in range(2):
                for tp in range(2):
                    cast(n, h, 2 * b + tp, on_vector)

        def store(n, which, dram, tile4):
            lo, hi = 2 * which[0], 2 * which[-1] + 2
            nc.sync.dma_start(
                out=dram[2 * n : 2 * n + 2].rearrange("h (m t) d -> m h t d", t=4)[:, :, lo:hi, :].rearrange(
                    "m h t d -> m h (t d)"
                ),
                in_=tile4[:, :, lo:hi, :].rearrange("p h t d -> p h (t d)"),
            )

        def store0(n, which):
            store(n, which, out_0, outs[n][0])

        def store1(n, which):
            store(n, which, out_1, outs[n][1][:].bitcast(U8))

        y_last = const.tile([P, 4, D], F32, name="y_last")
        last_stats = const.tile([P, 3, 4], F32, name="last_stats")

        def gain_last():
            nc.vector.tensor_tensor(
                out=y_last[:], in0=accs[(7, 1)][:].rearrange("p t (h d) -> p (t h) d", h=2),
                in1=gain[:].unsqueeze(1).broadcast_to([P, 4, D]), op=ALU.mult,
            )

        def scale_last():
            for c in range(4):
                nc.scalar.activation(
                    out=outs[7][0][:, c % 2, 2 + c // 2, :], in_=y_last[:, c, :], func=ACT.Copy,
                    scale=stats[7][1][:, 4 + c : 5 + c],
                )

        def peak_last():
            nc.vector.tensor_reduce(
                out=last_stats[:, 0, :], in_=y_last[:], axis=AX.X, op=ALU.max, apply_absolute_value=True,
            )

        def inverse_last():
            nc.vector.reciprocal(out=last_stats[:, 1, :], in_=last_stats[:, 0, :])

        def factor_last():
            nc.scalar.mul(out=last_stats[:, 2, :], in_=last_stats[:, 1, :], mul=448.0)

        def casts_last():
            for c in range(4):
                nc.vector.tensor_scalar(
                    out=outs[7][1][:, c % 2, 2 + c // 2, :], in0=y_last[:, c, :], scalar1=last_stats[:, 2, c : c + 1],
                    scalar2=None, op0=ALU.mult, saturate=False,
                )

        with tc.manual_schedule():
            transposes(0, ALL)
            copies(0, ALL)
            transposes(2, ALL)
            for g in ALL:
                quantize(0, g)
            copies(2, ALL)
            transposes(1, ALL)
            for g in ALL:
                quantize(2, g)
            copies(1, ALL)
            spread = psum_a.tile([P, 2, 256], F32, name="acc", tag="acc")
            nc.tensor.matmul(out=spread[:, 0, 0:D], lhsT=ones[:], rhs=gain_row[:], start=True, stop=True)
            matmuls(0, (0,))
            squares(0, 0)
            for g in ALL:
                quantize(1, g)
            nc.vector.tensor_copy(out=gain[:], in_=spread[:, 0, 0:D])

            for s in range(N_UNITS - 1):
                nxt, u, v = s + 3, s - 1, s - 2
                transposes(nxt, ALL)
                if s == 0:
                    matmuls(0, (1,))
                else:
                    matmuls(s, BOTH)
                last = s == N_UNITS - 2
                if u >= 0:
                    squares(u, 1)
                if last:
                    casts(v, (7,), False)
                else:
                    copies(nxt, (0,))
                if u >= 0:
                    rsqrt(u, 1)
                else:
                    rsqrt(0, 0)
                copies(nxt, ALL if last else (1, 2, 3))
                if s > 0:
                    squares(s, 0)
                    rsqrt(s, 0)
                if u >= 0:
                    normalize(u, 0)
                if v >= 0:
                    casts(v, (0, 1, 2, 3, 4, 5, 6) if last else (0, 1, 2, 3, 4, 5, 6, 7), True)
                    store1(v, BOTH)
                if u >= 0:
                    normalize(u, 1)
                    store0(u, BOTH)
                if last:
                    peak(u, (0,))
                quantize(nxt, 0)
                if last:
                    peak(u, (1,))
                elif u >= 0:
                    peak(u, BOTH)
                quantize(nxt, 1)
                if u >= 0:
                    inverse(u, BOTH)
                quantize(nxt, 2)
                if u >= 0:
                    factor(u, BOTH)
                quantize(nxt, 3)

            matmuls(7, BOTH)
            squares(6, 1)
            casts(5, (4,), False)
            rsqrt(6, 1)
            casts(5, (5, 6), False)
            squares(7, 0)
            rsqrt(7, 0)
            squares(7, 1)
            casts(5, (7,), False)
            rsqrt(7, 1)
            casts(5, (0, 1), True)
            normalize(6, 0)
            casts(5, (2, 3), True)
            peak(6, (0,))
            normalize(6, 1)
            store0(6, BOTH)
            store1(5, BOTH)
            inverse(6, (0,))
            peak(6, (1,))
            factor(6, (0,))
            normalize(7, 0)
            store0(7, (0,))
            casts(6, (0,), False)
            inverse(6, (1,))
            gain_last()
            scale_last()
            store0(7, (1,))
            casts(6, (1, 4), False)
            factor(6, (1,))
            peak(7, (0,))
            peak_last()
            inverse(7, (0,))
            factor_scalar(7, (0,))
            casts(6, (5,), False)
            casts(6, (6, 7), True)
            inverse_last()
            factor_last()
            casts(6, (2, 3), False)
            store1(6, BOTH)
            casts_bank(7, 0, True)
            casts_last()
            store1(7, BOTH)
